import numpy as np
import ml_dtypes


def mxq(x, axis, fmt="e4m3"):
    dtype, down = {"e4m3": (ml_dtypes.float8_e4m3fn, 7), "e5m2": (ml_dtypes.float8_e5m2, 14)}[fmt]
    v = np.moveaxis(np.asarray(x, np.float32).astype(ml_dtypes.bfloat16).astype(np.float64), axis, -1)
    blocks = v.reshape(v.shape[:-1] + (-1, 32))
    amax = np.abs(blocks).max(-1, keepdims=True)
    byte = np.maximum(np.where(amax > 0, np.frexp(amax)[1] - 1 + 127, 0) - down, 1)
    scale = np.exp2(byte - 127.0)
    codes = (blocks / scale).astype(np.float32).astype(dtype).astype(np.float64)
    return np.moveaxis((codes * scale).reshape(v.shape), -1, axis)


WIDE = False


def mx_kscale(k):
    if not WIDE:
        return np.ones(k)
    levels = np.array([10, -10, 5, -5, 0])
    a = np.random.permutation(np.resize(levels, k // 512 * 4)).reshape(k // 512, 4)
    idx = np.arange(k)
    return np.exp2(a[idx // 512, idx % 128 // 32])


BF16 = ml_dtypes.bfloat16


def bf(x):
    return np.asarray(x, np.float32).astype(BF16)


def f64(x):
    return np.asarray(x).astype(np.float64)


E2M1 = np.array([0.0, 0.5, 1.0, 1.5, 2.0, 3.0, 4.0, 6.0, -0.0, -0.5, -1.0, -1.5, -2.0, -3.0, -4.0, -6.0])


def pack_weight(w, fmt):
    k, n = w.shape
    w = f64(bf(w)).reshape(k // 32, 32, n)
    amax = np.abs(w).max(1)
    if fmt == "e4m3":
        byte = np.frexp(amax)[1] - 1 + 127 - 7
    else:
        mant, ex = np.frexp(amax / 6.0)
        byte = np.where(mant > 0.5, ex, ex - 1) + 127
    byte = np.clip(np.where(amax > 0, byte, 1), 1, 254)
    scaled = (w * np.exp2(127.0 - byte)[:, None, :]).reshape(k, n).astype(np.float32)
    by_word = np.ascontiguousarray(scaled.reshape(k // 512, 128, 4, n).transpose(0, 1, 3, 2))
    if fmt == "e4m3":
        words = by_word.astype(ml_dtypes.float8_e4m3fn).view(np.uint8)
    else:
        c = by_word.astype(ml_dtypes.float4_e2m1fn).view(np.uint8) & 0xF
        words = c[..., 0::2] | (c[..., 1::2] << 4)
    return np.ascontiguousarray(words), np.ascontiguousarray(byte.astype(np.uint8).reshape(k // 512, 16, n))


def unpack_weight(words, scales, fmt):
    g, p, n, _ = words.shape
    if fmt == "e4m3":
        vals = np.ascontiguousarray(words).view(ml_dtypes.float8_e4m3fn).astype(np.float64)
    else:
        nib = np.empty((g, p, n, 4), np.uint8)
        nib[..., 0::2] = words & 0xF
        nib[..., 1::2] = words >> 4
        vals = E2M1[nib]
    vals = vals * np.repeat(np.exp2(scales.astype(np.float64) - 127.0), 8, axis=1)[..., None]
    return vals.transpose(0, 1, 3, 2).reshape(g * 512, n)


B, S, M, D, H = 1, 128, 2, 2048, 6144
FMT = "e4m3"


def setup_inputs():
    s = mx_kscale(2 * D)
    lens = np.random.randint(0, M + 1, (B, S))
    valid = (np.arange(M)[None, None, :] < lens[:, :, None]).astype(np.float64)
    src = np.random.standard_normal((B, S, M, D)) / np.sqrt(M) * s[:D]
    neigh = np.random.standard_normal((B, S, M, D)) * 2.0 * valid[..., None] * s[D:]
    words, scales = pack_weight(np.random.standard_normal((2 * D, H)) / np.sqrt(2 * D) / s[:, None], FMT)
    return {"src_node_features": bf(src), "neigh_node_features": bf(neigh),
            "W_map_words": words, "W_map_scales": scales,
            "b_map": bf(-0.5 + 0.3 * np.random.standard_normal(H))}


def reference(src_node_features, neigh_node_features, W_map_words, W_map_scales, b_map):
    src, neigh = f64(src_node_features), f64(neigh_node_features)
    valid = np.any(neigh != 0, axis=-1)
    num = np.sum(valid, axis=-1).astype(np.float64)
    neigh_mean = neigh.sum(axis=2) / np.maximum(num, 1.0)[..., None]
    hidden = np.concatenate([src.sum(axis=2), neigh_mean], axis=-1)
    hidden = hidden.reshape(-1, hidden.shape[-1])
    v = (mxq(hidden, 1, "e4m3") @ unpack_weight(W_map_words, W_map_scales, FMT)) + f64(b_map)
    return np.where(v >= 0, v, 0.01 * v)

@@ -1,0 +1,269 @@
+from contextlib import ExitStack
+
+import concourse.mybir as mybir
+from concourse.masks import make_identity
+
+F32 = mybir.dt.float32
+BF16 = mybir.dt.bfloat16
+I32 = mybir.dt.int32
+U32 = mybir.dt.uint32
+U8 = mybir.dt.uint8
+FP8X4 = mybir.dt.float8_e4m3fn_x4
+ALU = mybir.AluOpType
+ACT = mybir.ActivationFunctionType
+
+P = 128
+D = 2048
+H = 6144
+G = 8
+NB = 512
+R1_BANKS = 8
+R1_COLS = R1_BANKS * NB
+R2_BANKS = 4
+R2_COLS = R2_BANKS * NB
+W_BUFS = 6
+PREFETCH = 5
+SCALES_ON_GPSIMD = False
+MANUAL = True
+
+FLOPS = 2 * P * (2 * D) * H
+
+
+def tile_syntacticgcn_w_kernel(
+    tc, src_node_features, neigh_node_features, W_map_words, W_map_scales, b_map, out
+):
+    nc = tc.nc
+    with ExitStack() as ctx:
+        if MANUAL:
+            ctx.enter_context(tc.manual_schedule())
+        const = ctx.enter_context(tc.tile_pool(name="const", bufs=1))
+        head = ctx.enter_context(tc.tile_pool(name="head", bufs=1))
+        wpool = ctx.enter_context(tc.tile_pool(name="wpool", bufs=W_BUFS))
+        spool = ctx.enter_context(tc.tile_pool(name="spool", bufs=R2_BANKS))
+        psum = ctx.enter_context(tc.psum_pool(name="psum", bufs=8))
+
+        ident = const.tile([P, P], BF16, name="ident")
+        bstage = const.tile([P, 3 * NB], BF16, name="bstage")
+        planes = [
+            const.tile([P, H], U8, name="planes%d" % j, align_bytes=64) for j in range(2)
+        ]
+        bias_sb = const.tile([P, H], BF16, name="bias_sb")
+        hcodes = const.tile([P, G * P], U32, name="hcodes", align_bytes=64)
+        hplanes = const.tile([P, G * P], U8, name="hplanes", align_bytes=64)
+        out_sb = const.tile([P, H], F32, name="out_sb")
+        asum = const.tile([P, 2], F32, name="asum")
+        valid = const.tile([P, 2], F32, name="valid")
+        num = const.tile([P, 1], F32, name="num")
+        rnum = const.tile([P, 1], F32, name="rnum")
+
+        neigh_sb = head.tile([P, 2, D], BF16, name="neigh_sb")
+        src_sb = head.tile([P, 2, D], BF16, name="src_sb")
+        junk = head.tile([P, D], BF16, name="junk")
+        nsum = head.tile([P, D], F32, name="nsum")
+        hs = head.tile([P, G, 4, P], BF16, name="hs")
+        grouped = head.tile([P, G, P, 4], BF16, name="grouped", align_bytes=64)
+
+        make_identity(nc, ident[:])
+        nc.vector.memset(bstage[:].bitcast(I32), 0)
+        nc.sync.dma_start(
+            out=neigh_sb[:], in_=neigh_node_features.rearrange("b s m d -> (b s) m d")
+        )
+        nc.sync.dma_start(out=bstage[0:4, :], in_=b_map.rearrange("(j n) -> j n", j=4))
+        nc.sync.dma_start(
+            out=src_sb[:], in_=src_node_features.rearrange("b s m d -> (b s) m d")
+        )
+        for j in range(2):
+            nc.vector.memset(planes[j][:].bitcast(I32), 0)
+        for j in range(2):
+            for q in range(4):
+                dst = planes[j][32 * q : 32 * q + 16, :]
+                srcv = W_map_scales[4 * j : 4 * j + 4, 4 * q : 4 * q + 4, :]
+                if SCALES_ON_GPSIMD:
+                    nc.gpsimd.dma_start(out=dst.bitcast(F32), in_=srcv.bitcast(F32))
+                else:
+                    nc.sync.dma_start(out=dst.bitcast(I32), in_=srcv.bitcast(I32))
+
+        loads = []
+        for g in range(G):
+            loads.append(("r1", g))
+        for g in range(0, 6, 2):
+            loads.append(("r2", g))
+        wtiles = {}
+
+        def issue_load(i):
+            kind, g = loads[i]
+            if kind == "r1":
+                wt = wpool.tile([P, R1_COLS], U32, name="wt%d" % i, tag="w", align_bytes=64)
+                nc.sync.dma_start(
+                    out=wt[:].bitcast(I32),
+                    in_=W_map_words[g]
+                    .rearrange("p n t -> p (n t)")[:, 0 : 4 * R1_COLS]
+                    .bitcast(I32),
+                )
+            else:
+                wt = wpool.tile([P, 2, R2_COLS], U32, name="wt%d" % i, tag="w", align_bytes=64)
+                nc.sync.dma_start(
+                    out=wt[:].bitcast(I32),
+                    in_=W_map_words[g : g + 2]
+                    .rearrange("g p n t -> p g (n t)")[:, :, 4 * R1_COLS : 4 * H]
+                    .bitcast(I32),
+                )
+            wtiles[i] = wt
+
+        stairs = []
+
+        def issue_stairs():
+            for s in range(R2_BANKS):
+                c0 = R1_COLS + NB * s
+                st = spool.tile([P, 2, NB], U32, name="st%d" % s, tag="s", align_bytes=64)
+                nc.sync.dma_start(
+                    out=st[:].bitcast(I32),
+                    in_=W_map_words[6:8]
+                    .rearrange("g p n t -> p g (n t)")[:, :, 4 * c0 : 4 * (c0 + NB)]
+                    .bitcast(I32),
+                )
+                stairs.append(st)
+
+        for i in range(PREFETCH):
+            issue_load(i)
+
+        def bias_bank(i, engine):
+            bp = psum.tile([P, NB], F32, name="bp%d" % i, tag="bank")
+            j, c = i // 3, i % 3
+            nc.tensor.matmul(
+                out=bp[:],
+                lhsT=ident[:, j : j + 1].to_broadcast([P, P]),
+                rhs=bstage[:, NB * c : NB * (c + 1)],
+                start=True,
+                stop=True,
+            )
+            if engine == "v":
+                nc.vector.tensor_copy(out=bias_sb[:, NB * i : NB * (i + 1)], in_=bp[:])
+            else:
+                nc.scalar.copy(out=bias_sb[:, NB * i : NB * (i + 1)], in_=bp[:])
+
+        for i in range(4):
+            bias_bank(i, "v")
+
+        for m in range(2):
+            nc.scalar.activation(
+                out=junk[:], in_=neigh_sb[:, m, :], func=ACT.Abs, accum_out=asum[:, m : m + 1]
+            )
+        nc.vector.tensor_tensor(out=nsum[:], in0=neigh_sb[:, 0, :], in1=neigh_sb[:, 1, :], op=ALU.add)
+
+        for i in range(4, 12):
+            bias_bank(i, "s")
+
+        def sorted_view(ap):
+            return ap.rearrange("n (g p t) -> n g t p", g=4, p=P, t=4)
+
+        def transposes(g0):
+            tp = psum.tile([P, 2, 4, P], BF16, name="tp%d" % g0, tag="bank")
+            for gg in range(2):
+                for t in range(4):
+                    nc.tensor.transpose(tp[:, gg, t, :], hs[:, g0 + gg, t, :], ident[:])
+            return tp
+
+        nc.vector.tensor_tensor(
+            out=hs[:, 0:4],
+            in0=sorted_view(src_sb[:, 0, :]),
+            in1=sorted_view(src_sb[:, 1, :]),
+            op=ALU.add,
+        )
+        tps = [transposes(0), transposes(2)]
+
+        nc.vector.tensor_single_scalar(out=valid[:], in_=asum[:], scalar=0.0, op=ALU.is_gt)
+        nc.vector.tensor_scalar(
+            out=num[:],
+            in0=valid[:, 0:1],
+            scalar1=valid[:, 1:2],
+            scalar2=1.0,
+            op0=ALU.add,
+            op1=ALU.max,
+        )
+        nc.vector.reciprocal(out=rnum[:], in_=num[:])
+        nc.vector.tensor_scalar(
+            out=hs[:, 4:8], in0=sorted_view(nsum[:]), scalar1=rnum[:, 0:1], scalar2=None, op0=ALU.mult
+        )
+        tps.append(transposes(4))
+        tps.append(transposes(6))
+
+        def copy_out(k, engine):
+            dst = grouped[:, 2 * k : 2 * k + 2]
+            srcv = tps[k][:].rearrange("p g t n -> p g n t")
+            if engine == "v":
+                nc.vector.tensor_copy(out=dst, in_=srcv)
+            else:
+                nc.scalar.copy(out=dst, in_=srcv)
+
+        def quantise(h):
+            nc.vector.quantize_mx(
+                out=hcodes[:, 4 * P * h : 4 * P * (h + 1)].bitcast(FP8X4),
+                scales=hplanes[:, 4 * P * h : 4 * P * (h + 1)],
+                in_=grouped[:, 4 * h : 4 * h + 4].rearrange("p g n t -> p (g n t)"),
+            )
+
+        copy_out(0, "v")
+        copy_out(1, "v")
+        copy_out(2, "s")
+        copy_out(3, "s")
+        quantise(0)
+        quantise(1)
+
+        def mx(acc, g, rhs, bank):
+            k = 4 * (g % 4)
+            nc.tensor.matmul_mx(
+                out=acc[:],
+                lhsT=hcodes[:, P * g : P * (g + 1)].bitcast(FP8X4),
+                lhsT_scale=hplanes[:, P * g : P * (g + 1)],
+                rhs=rhs.bitcast(FP8X4),
+                rhs_scale=planes[g // 4][k:P, NB * bank : NB * (bank + 1)],
+                start=(g == 0),
+                stop=(g == G - 1),
+            )
+
+        def add_bias(acc, bank):
+            cols = slice(NB * bank, NB * (bank + 1))
+            nc.vector.tensor_tensor(out=out_sb[:, cols], in0=acc[:], in1=bias_sb[:, cols], op=ALU.add)
+
+        def leaky_and_store(c0, c1):
+            nc.vector.scalar_tensor_tensor(
+                out=out_sb[:, c0:c1],
+                in0=out_sb[:, c0:c1],
+                scalar=0.01,
+                in1=out_sb[:, c0:c1],
+                op0=ALU.mult,
+                op1=ALU.max,
+            )
+            nc.scalar.dma_start(out=out[:, c0:c1], in_=out_sb[:, c0:c1])
+
+        accs = [psum.tile([P, NB], F32, name="acc%d" % b, tag="bank") for b in range(R1_BANKS)]
+        nxt = PREFETCH
+        for g in range(G):
+            if nxt < len(loads):
+                issue_load(nxt)
+                nxt += 1
+            elif not stairs:
+                issue_stairs()
+            for b in range(R1_BANKS):
+                mx(accs[b], g, wtiles[g][:, NB * b : NB * (b + 1)], b)
+
+        for half in range(2):
+            for b in range(4 * half, 4 * half + 4):
+                add_bias(accs[b], b)
+            leaky_and_store(4 * NB * half, 4 * NB * (half + 1))
+
+        accs2 = [
+            psum.tile([P, NB], F32, name="acc%d" % (R1_BANKS + b), tag="bank") for b in range(R2_BANKS)
+        ]
+        for i in range(G, len(loads)):
+            g0 = loads[i][1]
+            for gg in range(2):
+                for b in range(R2_BANKS):
+                    mx(accs2[b], g0 + gg, wtiles[i][:, gg, NB * b : NB * (b + 1)], R1_BANKS + b)
+        for s in range(R2_BANKS):
+            for gg in range(2):
+                mx(accs2[s], 6 + gg, stairs[s][:, gg, :], R1_BANKS + s)
+            add_bias(accs2[s], R1_BANKS + s)
+            c0 = R1_COLS + NB * s
+            leaky_and_store(c0, c0 + NB)

@@ -23,7 +23,7 @@ R2_BANKS = 4
 R2_COLS = R2_BANKS * NB
 W_BUFS = 6
 PREFETCH = 5
-SCALES_ON_GPSIMD = False
+SCALES_ON_GPSIMD = True
 MANUAL = True
 
 FLOPS = 2 * P * (2 * D) * H

@@ -17,14 +17,12 @@ D = 2048
 H = 6144
 G = 8
 NB = 512
-R1_BANKS = 8
-R1_COLS = R1_BANKS * NB
-R2_BANKS = 4
-R2_COLS = R2_BANKS * NB
-W_BUFS = 6
-PREFETCH = 5
-SCALES_ON_GPSIMD = True
-MANUAL = True
+RB = 4
+RC = RB * NB
+ROUNDS = 3
+STAIR_G = 2
+W_BUFS = 12
+PREFETCH = 11
 
 FLOPS = 2 * P * (2 * D) * H
 
@@ -34,13 +32,13 @@ def tile_syntacticgcn_w_kernel(
 ):
     nc = tc.nc
     with ExitStack() as ctx:
-        if MANUAL:
-            ctx.enter_context(tc.manual_schedule())
+        ctx.enter_context(tc.manual_schedule())
         const = ctx.enter_context(tc.tile_pool(name="const", bufs=1))
         head = ctx.enter_context(tc.tile_pool(name="head", bufs=1))
         wpool = ctx.enter_context(tc.tile_pool(name="wpool", bufs=W_BUFS))
-        spool = ctx.enter_context(tc.tile_pool(name="spool", bufs=R2_BANKS))
-        psum = ctx.enter_context(tc.psum_pool(name="psum", bufs=8))
+        spool = ctx.enter_context(tc.tile_pool(name="spool", bufs=RB))
+        accp = ctx.enter_context(tc.psum_pool(name="accp", bufs=6))
+        auxp = ctx.enter_context(tc.psum_pool(name="auxp", bufs=2))
 
         ident = const.tile([P, P], BF16, name="ident")
         bstage = const.tile([P, 3 * NB], BF16, name="bstage")
@@ -64,61 +62,49 @@ def tile_syntacticgcn_w_kernel(
         grouped = head.tile([P, G, P, 4], BF16, name="grouped", align_bytes=64)
 
         make_identity(nc, ident[:])
+        for j in range(2):
+            nc.vector.memset(planes[j][:].bitcast(I32), 0)
         nc.vector.memset(bstage[:].bitcast(I32), 0)
+        nc.sync.dma_start(
+            out=src_sb[:], in_=src_node_features.rearrange("b s m d -> (b s) m d")
+        )
         nc.sync.dma_start(
             out=neigh_sb[:], in_=neigh_node_features.rearrange("b s m d -> (b s) m d")
         )
         nc.sync.dma_start(out=bstage[0:4, :], in_=b_map.rearrange("(j n) -> j n", j=4))
-        nc.sync.dma_start(
-            out=src_sb[:], in_=src_node_features.rearrange("b s m d -> (b s) m d")
-        )
-        for j in range(2):
-            nc.vector.memset(planes[j][:].bitcast(I32), 0)
         for j in range(2):
             for q in range(4):
-                dst = planes[j][32 * q : 32 * q + 16, :]
-                srcv = W_map_scales[4 * j : 4 * j + 4, 4 * q : 4 * q + 4, :]
-                if SCALES_ON_GPSIMD:
-                    nc.gpsimd.dma_start(out=dst.bitcast(F32), in_=srcv.bitcast(F32))
-                else:
-                    nc.sync.dma_start(out=dst.bitcast(I32), in_=srcv.bitcast(I32))
+                nc.gpsimd.dma_start(
+                    out=planes[j][32 * q : 32 * q + 16, :].bitcast(F32),
+                    in_=W_map_scales[4 * j : 4 * j + 4, 4 * q : 4 * q + 4, :].bitcast(F32),
+                )
 
         loads = []
-        for g in range(G):
-            loads.append(("r1", g))
-        for g in range(0, 6, 2):
-            loads.append(("r2", g))
+        for r in range(ROUNDS):
+            for g in range(G):
+                if r < ROUNDS - 1 or g < G - STAIR_G:
+                    loads.append((r, g))
         wtiles = {}
-
-        def issue_load(i):
-            kind, g = loads[i]
-            if kind == "r1":
-                wt = wpool.tile([P, R1_COLS], U32, name="wt%d" % i, tag="w", align_bytes=64)
-                nc.sync.dma_start(
-                    out=wt[:].bitcast(I32),
-                    in_=W_map_words[g]
-                    .rearrange("p n t -> p (n t)")[:, 0 : 4 * R1_COLS]
-                    .bitcast(I32),
-                )
-            else:
-                wt = wpool.tile([P, 2, R2_COLS], U32, name="wt%d" % i, tag="w", align_bytes=64)
-                nc.sync.dma_start(
-                    out=wt[:].bitcast(I32),
-                    in_=W_map_words[g : g + 2]
-                    .rearrange("g p n t -> p g (n t)")[:, :, 4 * R1_COLS : 4 * H]
-                    .bitcast(I32),
-                )
-            wtiles[i] = wt
-
         stairs = []
 
+        def issue_load(i):
+            r, g = loads[i]
+            wt = wpool.tile([P, RC], U32, name="wt%d" % i, tag="w", align_bytes=64)
+            nc.sync.dma_start(
+                out=wt[:].bitcast(I32),
+                in_=W_map_words[g]
+                .rearrange("p n t -> p (n t)")[:, 4 * RC * r : 4 * RC * (r + 1)]
+                .bitcast(I32),
+            )
+            wtiles[i] = wt
+
         def issue_stairs():
-            for s in range(R2_BANKS):
-                c0 = R1_COLS + NB * s
-                st = spool.tile([P, 2, NB], U32, name="st%d" % s, tag="s", align_bytes=64)
+            for s in range(RB):
+                c0 = RC * (ROUNDS - 1) + NB * s
+                st = spool.tile([P, STAIR_G, NB], U32, name="st%d" % s, tag="s", align_bytes=64)
                 nc.sync.dma_start(
                     out=st[:].bitcast(I32),
-                    in_=W_map_words[6:8]
+                    in_=W_map_words[G - STAIR_G : G]
                     .rearrange("g p n t -> p g (n t)")[:, :, 4 * c0 : 4 * (c0 + NB)]
                     .bitcast(I32),
                 )
@@ -127,70 +113,19 @@ def tile_syntacticgcn_w_kernel(
         for i in range(PREFETCH):
             issue_load(i)
 
-        def bias_bank(i, engine):
-            bp = psum.tile([P, NB], F32, name="bp%d" % i, tag="bank")
-            j, c = i // 3, i % 3
-            nc.tensor.matmul(
-                out=bp[:],
-                lhsT=ident[:, j : j + 1].to_broadcast([P, P]),
-                rhs=bstage[:, NB * c : NB * (c + 1)],
-                start=True,
-                stop=True,
-            )
-            if engine == "v":
-                nc.vector.tensor_copy(out=bias_sb[:, NB * i : NB * (i + 1)], in_=bp[:])
-            else:
-                nc.scalar.copy(out=bias_sb[:, NB * i : NB * (i + 1)], in_=bp[:])
-
-        for i in range(4):
-            bias_bank(i, "v")
-
-        for m in range(2):
-            nc.scalar.activation(
-                out=junk[:], in_=neigh_sb[:, m, :], func=ACT.Abs, accum_out=asum[:, m : m + 1]
-            )
-        nc.vector.tensor_tensor(out=nsum[:], in0=neigh_sb[:, 0, :], in1=neigh_sb[:, 1, :], op=ALU.add)
-
-        for i in range(4, 12):
-            bias_bank(i, "s")
-
-        def sorted_view(ap):
-            return ap.rearrange("n (g p t) -> n g t p", g=4, p=P, t=4)
+        def sorted_view(ap, g):
+            return ap.rearrange("n (g p t) -> n g t p", g=g, p=P, t=4)
 
         def transposes(g0):
-            tp = psum.tile([P, 2, 4, P], BF16, name="tp%d" % g0, tag="bank")
+            tp = auxp.tile([P, 2, 4, P], BF16, name="tp%d" % g0, tag="aux")
             for gg in range(2):
                 for t in range(4):
                     nc.tensor.transpose(tp[:, gg, t, :], hs[:, g0 + gg, t, :], ident[:])
             return tp
 
-        nc.vector.tensor_tensor(
-            out=hs[:, 0:4],
-            in0=sorted_view(src_sb[:, 0, :]),
-            in1=sorted_view(src_sb[:, 1, :]),
-            op=ALU.add,
-        )
-        tps = [transposes(0), transposes(2)]
-
-        nc.vector.tensor_single_scalar(out=valid[:], in_=asum[:], scalar=0.0, op=ALU.is_gt)
-        nc.vector.tensor_scalar(
-            out=num[:],
-            in0=valid[:, 0:1],
-            scalar1=valid[:, 1:2],
-            scalar2=1.0,
-            op0=ALU.add,
-            op1=ALU.max,
-        )
-        nc.vector.reciprocal(out=rnum[:], in_=num[:])
-        nc.vector.tensor_scalar(
-            out=hs[:, 4:8], in0=sorted_view(nsum[:]), scalar1=rnum[:, 0:1], scalar2=None, op0=ALU.mult
-        )
-        tps.append(transposes(4))
-        tps.append(transposes(6))
-
-        def copy_out(k, engine):
-            dst = grouped[:, 2 * k : 2 * k + 2]
-            srcv = tps[k][:].rearrange("p g t n -> p g n t")
+        def copy_out(tp, g0, engine):
+            dst = grouped[:, g0 : g0 + 2]
+            srcv = tp[:].rearrange("p g t n -> p g n t")
             if engine == "v":
                 nc.vector.tensor_copy(out=dst, in_=srcv)
             else:
@@ -203,12 +138,57 @@ def tile_syntacticgcn_w_kernel(
                 in_=grouped[:, 4 * h : 4 * h + 4].rearrange("p g n t -> p (g n t)"),
             )
 
-        copy_out(0, "v")
-        copy_out(1, "v")
-        copy_out(2, "s")
-        copy_out(3, "s")
+        tps = []
+        for k in range(2):
+            cols = slice(1024 * k, 1024 * (k + 1))
+            nc.vector.tensor_tensor(
+                out=hs[:, 2 * k : 2 * k + 2],
+                in0=sorted_view(src_sb[:, 0, cols], 2),
+                in1=sorted_view(src_sb[:, 1, cols], 2),
+                op=ALU.add,
+            )
+            tps.append(transposes(2 * k))
+        copy_out(tps[0], 0, "v")
+        copy_out(tps[1], 2, "v")
         quantise(0)
-        quantise(1)
+
+        for m in range(2):
+            nc.scalar.activation(
+                out=junk[:], in_=neigh_sb[:, m, :], func=ACT.Abs, accum_out=asum[:, m : m + 1]
+            )
+        nc.vector.tensor_tensor(out=nsum[:], in0=neigh_sb[:, 0, :], in1=neigh_sb[:, 1, :], op=ALU.add)
+        nc.vector.tensor_single_scalar(out=valid[:], in_=asum[:], scalar=0.0, op=ALU.is_gt)
+        nc.vector.tensor_scalar(
+            out=num[:],
+            in0=valid[:, 0:1],
+            scalar1=valid[:, 1:2],
+            scalar2=1.0,
+            op0=ALU.add,
+            op1=ALU.max,
+        )
+        nc.vector.reciprocal(out=rnum[:], in_=num[:])
+        nc.vector.tensor_scalar(
+            out=hs[:, 4:8], in0=sorted_view(nsum[:], 4), scalar1=rnum[:, 0:1], scalar2=None, op0=ALU.mult
+        )
+
+        def second_half():
+            t4 = transposes(4)
+            t6 = transposes(6)
+            copy_out(t4, 4, "v")
+            copy_out(t6, 6, "s")
+            quantise(1)
+
+        def bias_bank(i):
+            bp = auxp.tile([P, NB], F32, name="bp%d" % i, tag="aux")
+            j, c = i // 3, i % 3
+            nc.tensor.matmul(
+                out=bp[:],
+                lhsT=ident[:, j : j + 1].to_broadcast([P, P]),
+                rhs=bstage[:, NB * c : NB * (c + 1)],
+                start=True,
+                stop=True,
+            )
+            nc.scalar.copy(out=bias_sb[:, NB * i : NB * (i + 1)], in_=bp[:])
 
         def mx(acc, g, rhs, bank):
             k = 4 * (g % 4)
@@ -237,33 +217,31 @@ def tile_syntacticgcn_w_kernel(
             )
             nc.scalar.dma_start(out=out[:, c0:c1], in_=out_sb[:, c0:c1])
 
-        accs = [psum.tile([P, NB], F32, name="acc%d" % b, tag="bank") for b in range(R1_BANKS)]
-        nxt = PREFETCH
-        for g in range(G):
-            if nxt < len(loads):
-                issue_load(nxt)
-                nxt += 1
-            elif not stairs:
+        accs = []
+        for i in range(len(loads)):
+            r, g = loads[i]
+            if i + PREFETCH < len(loads):
+                issue_load(i + PREFETCH)
+            elif i + PREFETCH == len(loads):
                 issue_stairs()
-            for b in range(R1_BANKS):
-                mx(accs[b], g, wtiles[g][:, NB * b : NB * (b + 1)], b)
+            if g == 0:
+                accs = [
+                    accp.tile([P, NB], F32, name="acc%d" % (RB * r + b), tag="acc") for b in range(RB)
+                ]
+            if i == 4:
+                second_half()
+            for b in range(RB):
+                mx(accs[b], g, wtiles[i][:, NB * b : NB * (b + 1)], RB * r + b)
+            if 2 <= i < 14:
+                bias_bank(i - 2)
+            if g == G - 1:
+                for b in range(RB):
+                    add_bias(accs[b], RB * r + b)
+                leaky_and_store(RC * r, RC * (r + 1))
 
-        for half in range(2):
-            for b in range(4 * half, 4 * half + 4):
-                add_bias(accs[b], b)
-            leaky_and_store(4 * NB * half, 4 * NB * (half + 1))
-
-        accs2 = [
-            psum.tile([P, NB], F32, name="acc%d" % (R1_BANKS + b), tag="bank") for b in range(R2_BANKS)
-        ]
-        for i in range(G, len(loads)):
-            g0 = loads[i][1]
-            for gg in range(2):
-                for b in range(R2_BANKS):
-                    mx(accs2[b], g0 + gg, wtiles[i][:, gg, NB * b : NB * (b + 1)], R1_BANKS + b)
-        for s in range(R2_BANKS):
-            for gg in range(2):
-                mx(accs2[s], 6 + gg, stairs[s][:, gg, :], R1_BANKS + s)
-            add_bias(accs2[s], R1_BANKS + s)
-            c0 = R1_COLS + NB * s
-            leaky_and_store(c0, c0 + NB)
+        for s in range(RB):
+            bank = RB * (ROUNDS - 1) + s
+            for gg in range(STAIR_G):
+                mx(accs[s], G - STAIR_G + gg, stairs[s][:, gg, :], bank)
+            add_bias(accs[s], bank)
+            leaky_and_store(NB * bank, NB * (bank + 1))

@@ -206,7 +206,7 @@ def tile_syntacticgcn_w_kernel(
             cols = slice(NB * bank, NB * (bank + 1))
             nc.vector.tensor_tensor(out=out_sb[:, cols], in0=acc[:], in1=bias_sb[:, cols], op=ALU.add)
 
-        def leaky_and_store(c0, c1):
+        def leaky(c0, c1):
             nc.vector.scalar_tensor_tensor(
                 out=out_sb[:, c0:c1],
                 in0=out_sb[:, c0:c1],
@@ -215,15 +215,20 @@ def tile_syntacticgcn_w_kernel(
                 op0=ALU.mult,
                 op1=ALU.max,
             )
-            nc.scalar.dma_start(out=out[:, c0:c1], in_=out_sb[:, c0:c1])
+
+        def store(c0, c1):
+            nc.sync.dma_start(out=out[:, c0:c1], in_=out_sb[:, c0:c1])
 
         accs = []
+        held_back = []
         for i in range(len(loads)):
             r, g = loads[i]
             if i + PREFETCH < len(loads):
                 issue_load(i + PREFETCH)
             elif i + PREFETCH == len(loads):
                 issue_stairs()
+                for c0, c1 in held_back:
+                    store(c0, c1)
             if g == 0:
                 accs = [
                     accp.tile([P, NB], F32, name="acc%d" % (RB * r + b), tag="acc") for b in range(RB)
@@ -237,11 +242,16 @@ def tile_syntacticgcn_w_kernel(
             if g == G - 1:
                 for b in range(RB):
                     add_bias(accs[b], RB * r + b)
-                leaky_and_store(RC * r, RC * (r + 1))
+                leaky(RC * r, RC * (r + 1))
+                if stairs:
+                    store(RC * r, RC * (r + 1))
+                else:
+                    held_back.append((RC * r, RC * (r + 1)))
 
         for s in range(RB):
             bank = RB * (ROUNDS - 1) + s
             for gg in range(STAIR_G):
                 mx(accs[s], G - STAIR_G + gg, stairs[s][:, gg, :], bank)
             add_bias(accs[s], bank)
-            leaky_and_store(NB * bank, NB * (bank + 1))
+            leaky(NB * bank, NB * (bank + 1))
+            store(NB * bank, NB * (bank + 1))

@@ -10,7 +10,6 @@ U32 = mybir.dt.uint32
 U8 = mybir.dt.uint8
 FP8X4 = mybir.dt.float8_e4m3fn_x4
 ALU = mybir.AluOpType
-ACT = mybir.ActivationFunctionType
 
 P = 128
 D = 2048
@@ -49,14 +48,14 @@ def tile_syntacticgcn_w_kernel(
         hcodes = const.tile([P, G * P], U32, name="hcodes", align_bytes=64)
         hplanes = const.tile([P, G * P], U8, name="hplanes", align_bytes=64)
         out_sb = const.tile([P, H], F32, name="out_sb")
-        asum = const.tile([P, 2], F32, name="asum")
+        maxbits = const.tile([P, 2], F32, name="maxbits")
         valid = const.tile([P, 2], F32, name="valid")
         num = const.tile([P, 1], F32, name="num")
         rnum = const.tile([P, 1], F32, name="rnum")
 
         neigh_sb = head.tile([P, 2, D], BF16, name="neigh_sb")
         src_sb = head.tile([P, 2, D], BF16, name="src_sb")
-        junk = head.tile([P, D], BF16, name="junk")
+        magbits = head.tile([P, 2, D // 2], I32, name="magbits")
         nsum = head.tile([P, D], F32, name="nsum")
         hs = head.tile([P, G, 4, P], BF16, name="hs")
         grouped = head.tile([P, G, P, 4], BF16, name="grouped", align_bytes=64)
@@ -152,12 +151,12 @@ def tile_syntacticgcn_w_kernel(
         copy_out(tps[1], 2, "v")
         quantise(0)
 
-        for m in range(2):
-            nc.scalar.activation(
-                out=junk[:], in_=neigh_sb[:, m, :], func=ACT.Abs, accum_out=asum[:, m : m + 1]
-            )
+        nc.vector.tensor_single_scalar(
+            out=magbits[:], in_=neigh_sb[:].bitcast(I32), scalar=0x7FFF7FFF, op=ALU.bitwise_and
+        )
+        nc.vector.tensor_reduce(out=maxbits[:], in_=magbits[:], axis=mybir.AxisListType.X, op=ALU.max)
         nc.vector.tensor_tensor(out=nsum[:], in0=neigh_sb[:, 0, :], in1=neigh_sb[:, 1, :], op=ALU.add)
-        nc.vector.tensor_single_scalar(out=valid[:], in_=asum[:], scalar=0.0, op=ALU.is_gt)
+        nc.vector.tensor_single_scalar(out=valid[:], in_=maxbits[:], scalar=0.0, op=ALU.is_gt)
         nc.vector.tensor_scalar(
             out=num[:],
             in0=valid[:, 0:1],
@@ -220,15 +219,12 @@ def tile_syntacticgcn_w_kernel(
             nc.sync.dma_start(out=out[:, c0:c1], in_=out_sb[:, c0:c1])
 
         accs = []
-        held_back = []
         for i in range(len(loads)):
             r, g = loads[i]
             if i + PREFETCH < len(loads):
                 issue_load(i + PREFETCH)
             elif i + PREFETCH == len(loads):
                 issue_stairs()
-                for c0, c1 in held_back:
-                    store(c0, c1)
             if g == 0:
                 accs = [
                     accp.tile([P, NB], F32, name="acc%d" % (RB * r + b), tag="acc") for b in range(RB)
@@ -243,10 +239,9 @@ def tile_syntacticgcn_w_kernel(
                 for b in range(RB):
                     add_bias(accs[b], RB * r + b)
                 leaky(RC * r, RC * (r + 1))
-                if stairs:
-                    store(RC * r, RC * (r + 1))
-                else:
-                    held_back.append((RC * r, RC * (r + 1)))
+                if r == ROUNDS - 2:
+                    assert stairs
+                    store(0, RC * (r + 1))
 
         for s in range(RB):
             bank = RB * (ROUNDS - 1) + s

@@ -16,12 +16,13 @@ D = 2048
 H = 6144
 G = 8
 NB = 512
-RB = 4
-RC = RB * NB
-ROUNDS = 3
-STAIR_G = 2
-W_BUFS = 12
-PREFETCH = 11
+AB = 8
+BB = 4
+PLAIN = 6
+AC = AB * NB
+BC = BB * NB
+STAIR = 2
+W_BUFS = 8
 
 FLOPS = 2 * P * (2 * D) * H
 
@@ -35,8 +36,7 @@ def tile_syntacticgcn_w_kernel(
         const = ctx.enter_context(tc.tile_pool(name="const", bufs=1))
         head = ctx.enter_context(tc.tile_pool(name="head", bufs=1))
         wpool = ctx.enter_context(tc.tile_pool(name="wpool", bufs=W_BUFS))
-        spool = ctx.enter_context(tc.tile_pool(name="spool", bufs=RB))
-        accp = ctx.enter_context(tc.psum_pool(name="accp", bufs=6))
+        accp = ctx.enter_context(tc.psum_pool(name="accp", bufs=PLAIN))
         auxp = ctx.enter_context(tc.psum_pool(name="auxp", bufs=2))
 
         ident = const.tile([P, P], BF16, name="ident")
@@ -78,39 +78,24 @@ def tile_syntacticgcn_w_kernel(
                     in_=W_map_scales[4 * j : 4 * j + 4, 4 * q : 4 * q + 4, :].bitcast(F32),
                 )
 
-        loads = []
-        for r in range(ROUNDS):
-            for g in range(G):
-                if r < ROUNDS - 1 or g < G - STAIR_G:
-                    loads.append((r, g))
-        wtiles = {}
-        stairs = []
+        pieces = {}
 
-        def issue_load(i):
-            r, g = loads[i]
-            wt = wpool.tile([P, RC], U32, name="wt%d" % i, tag="w", align_bytes=64)
+        def load(g0, n, b0, b1):
+            wt = wpool.tile(
+                [P, n, NB * (b1 - b0)], U32, name="w%d_%d" % (g0, b0), tag="w", align_bytes=64
+            )
             nc.sync.dma_start(
                 out=wt[:].bitcast(I32),
-                in_=W_map_words[g]
-                .rearrange("p n t -> p (n t)")[:, 4 * RC * r : 4 * RC * (r + 1)]
+                in_=W_map_words[g0 : g0 + n]
+                .rearrange("g p n t -> p g (n t)")[:, :, 4 * NB * b0 : 4 * NB * b1]
                 .bitcast(I32),
             )
-            wtiles[i] = wt
+            for b in range(b0, b1):
+                for gg in range(n):
+                    pieces[(g0 + gg, b)] = wt[:, gg, NB * (b - b0) : NB * (b - b0 + 1)]
 
-        def issue_stairs():
-            for s in range(RB):
-                c0 = RC * (ROUNDS - 1) + NB * s
-                st = spool.tile([P, STAIR_G, NB], U32, name="st%d" % s, tag="s", align_bytes=64)
-                nc.sync.dma_start(
-                    out=st[:].bitcast(I32),
-                    in_=W_map_words[G - STAIR_G : G]
-                    .rearrange("g p n t -> p g (n t)")[:, :, 4 * c0 : 4 * (c0 + NB)]
-                    .bitcast(I32),
-                )
-                stairs.append(st)
-
-        for i in range(PREFETCH):
-            issue_load(i)
+        for g in range(G):
+            load(g, 1, 0, AB)
 
         def sorted_view(ap, g):
             return ap.rearrange("n (g p t) -> n g t p", g=g, p=P, t=4)
@@ -189,13 +174,13 @@ def tile_syntacticgcn_w_kernel(
             )
             nc.scalar.copy(out=bias_sb[:, NB * i : NB * (i + 1)], in_=bp[:])
 
-        def mx(acc, g, rhs, bank):
+        def mx(acc, g, bank):
             k = 4 * (g % 4)
             nc.tensor.matmul_mx(
                 out=acc[:],
                 lhsT=hcodes[:, P * g : P * (g + 1)].bitcast(FP8X4),
                 lhsT_scale=hplanes[:, P * g : P * (g + 1)],
-                rhs=rhs.bitcast(FP8X4),
+                rhs=pieces[(g, bank)].bitcast(FP8X4),
                 rhs_scale=planes[g // 4][k:P, NB * bank : NB * (bank + 1)],
                 start=(g == 0),
                 stop=(g == G - 1),
@@ -218,35 +203,48 @@ def tile_syntacticgcn_w_kernel(
         def store(c0, c1):
             nc.sync.dma_start(out=out[:, c0:c1], in_=out_sb[:, c0:c1])
 
-        accs = []
-        for i in range(len(loads)):
-            r, g = loads[i]
-            if i + PREFETCH < len(loads):
-                issue_load(i + PREFETCH)
-            elif i + PREFETCH == len(loads):
-                issue_stairs()
-            if g == 0:
-                accs = [
-                    accp.tile([P, NB], F32, name="acc%d" % (RB * r + b), tag="acc") for b in range(RB)
-                ]
-            if i == 4:
-                second_half()
-            for b in range(RB):
-                mx(accs[b], g, wtiles[i][:, NB * b : NB * (b + 1)], RB * r + b)
-            if 2 <= i < 14:
-                bias_bank(i - 2)
-            if g == G - 1:
-                for b in range(RB):
-                    add_bias(accs[b], RB * r + b)
-                leaky(RC * r, RC * (r + 1))
-                if r == ROUNDS - 2:
-                    assert stairs
-                    store(0, RC * (r + 1))
+        def finish(accs, bank):
+            n = len(accs)
+            for b in range(n + 1):
+                if b < n:
+                    add_bias(accs[b], bank + b)
+                if b > 0:
+                    leaky(NB * (bank + b - 1), NB * (bank + b))
 
-        for s in range(RB):
-            bank = RB * (ROUNDS - 1) + s
-            for gg in range(STAIR_G):
-                mx(accs[s], G - STAIR_G + gg, stairs[s][:, gg, :], bank)
-            add_bias(accs[s], bank)
-            leaky(NB * bank, NB * (bank + 1))
-            store(NB * bank, NB * (bank + 1))
+        accs = [accp.tile([P, NB], F32, name="acc%d" % b, tag="acc") for b in range(PLAIN)]
+        for g in range(G):
+            if g == 4:
+                second_half()
+                accs += [auxp.tile([P, NB], F32, name="acc%d" % b, tag="aux") for b in range(PLAIN, AB)]
+                for b in range(PLAIN, AB):
+                    for gg in range(g):
+                        mx(accs[b], gg, b)
+            for b in range(len(accs)):
+                mx(accs[b], g, b)
+            if g < 4:
+                for i in range(3):
+                    bias_bank(3 * g + i)
+            if g == 4:
+                load(0, 2, AB, AB + BB)
+                load(2, 2, AB, AB + BB)
+                load(4, 2, AB, AB + BB)
+                for b in range(AB, AB + BB, STAIR):
+                    load(6, 2, b, b + STAIR)
+        finish(accs, 0)
+        store(0, AC)
+
+        accs = [accp.tile([P, NB], F32, name="acc%d" % (AB + b), tag="acc") for b in range(BB)]
+        for g0 in range(0, 6, 2):
+            for b in range(BB):
+                for g in range(g0, g0 + 2):
+                    mx(accs[b], g, AB + b)
+        for b0 in range(0, BB, STAIR):
+            for b in range(b0, b0 + STAIR):
+                for g in range(6, G):
+                    mx(accs[b], g, AB + b)
+            finish(accs[b0 : b0 + STAIR], AB + b0)
+            if b0 + STAIR < BB:
+                store(NB * (AB + b0), NB * (AB + b0 + STAIR))
+            else:
+                for b in range(AB + b0, AB + b0 + STAIR):
+                    store(NB * b, NB * (b + 1))

@@ -70,7 +70,6 @@ def tile_syntacticgcn_w_kernel(
         nc.sync.dma_start(
             out=neigh_sb[:], in_=neigh_node_features.rearrange("b s m d -> (b s) m d")
         )
-        nc.sync.dma_start(out=bstage[0:4, :], in_=b_map.rearrange("(j n) -> j n", j=4))
         for j in range(2):
             for q in range(4):
                 nc.gpsimd.dma_start(
@@ -96,6 +95,8 @@ def tile_syntacticgcn_w_kernel(
 
         for g in range(G):
             load(g, 1, 0, AB)
+            if g == 0:
+                nc.sync.dma_start(out=bstage[0:4, :], in_=b_map.rearrange("(j n) -> j n", j=4))
 
         def sorted_view(ap, g):
             return ap.rearrange("n (g p t) -> n g t p", g=g, p=P, t=4)

@@ -72,7 +72,7 @@ def tile_syntacticgcn_w_kernel(
         )
         for j in range(2):
             for q in range(4):
-                nc.gpsimd.dma_start(
+                (nc.scalar, nc.gpsimd)[j].dma_start(
                     out=planes[j][32 * q : 32 * q + 16, :].bitcast(F32),
                     in_=W_map_scales[4 * j : 4 * j + 4, 4 * q : 4 * q + 4, :].bitcast(F32),
                 )

from contextlib import ExitStack

import concourse.mybir as mybir
from concourse.masks import make_identity

F32 = mybir.dt.float32
BF16 = mybir.dt.bfloat16
I32 = mybir.dt.int32
U32 = mybir.dt.uint32
U8 = mybir.dt.uint8
FP8X4 = mybir.dt.float8_e4m3fn_x4
ALU = mybir.AluOpType

P = 128
D = 2048
H = 6144
G = 8
NB = 512
AB = 8
BB = 4
PLAIN = 6
AC = AB * NB
BC = BB * NB
STAIR = 2
W_BUFS = 8

FLOPS = 2 * P * (2 * D) * H


def tile_syntacticgcn_w_kernel(
    tc, src_node_features, neigh_node_features, W_map_words, W_map_scales, b_map, out
):
    nc = tc.nc
    with ExitStack() as ctx:
        ctx.enter_context(tc.manual_schedule())
        const = ctx.enter_context(tc.tile_pool(name="const", bufs=1))
        head = ctx.enter_context(tc.tile_pool(name="head", bufs=1))
        wpool = ctx.enter_context(tc.tile_pool(name="wpool", bufs=W_BUFS))
        accp = ctx.enter_context(tc.psum_pool(name="accp", bufs=PLAIN))
        auxp = ctx.enter_context(tc.psum_pool(name="auxp", bufs=2))

        ident = const.tile([P, P], BF16, name="ident")
        bstage = const.tile([P, 3 * NB], BF16, name="bstage")
        planes = [
            const.tile([P, H], U8, name="planes%d" % j, align_bytes=64) for j in range(2)
        ]
        bias_sb = const.tile([P, H], BF16, name="bias_sb")
        hcodes = const.tile([P, G * P], U32, name="hcodes", align_bytes=64)
        hplanes = const.tile([P, G * P], U8, name="hplanes", align_bytes=64)
        out_sb = const.tile([P, H], F32, name="out_sb")
        maxbits = const.tile([P, 2], F32, name="maxbits")
        valid = const.tile([P, 2], F32, name="valid")
        num = const.tile([P, 1], F32, name="num")
        rnum = const.tile([P, 1], F32, name="rnum")

        neigh_sb = head.tile([P, 2, D], BF16, name="neigh_sb")
        src_sb = head.tile([P, 2, D], BF16, name="src_sb")
        magbits = head.tile([P, 2, D // 2], I32, name="magbits")
        nsum = head.tile([P, D], F32, name="nsum")
        hs = head.tile([P, G, 4, P], BF16, name="hs")
        grouped = head.tile([P, G, P, 4], BF16, name="grouped", align_bytes=64)

        make_identity(nc, ident[:])
        for j in range(2):
            nc.vector.memset(planes[j][:].bitcast(I32), 0)
        nc.vector.memset(bstage[:].bitcast(I32), 0)
        nc.sync.dma_start(
            out=src_sb[:], in_=src_node_features.rearrange("b s m d -> (b s) m d")
        )
        nc.sync.dma_start(
            out=neigh_sb[:], in_=neigh_node_features.rearrange("b s m d -> (b s) m d")
        )
        for j in range(2):
            for q in range(4):
                (nc.scalar, nc.gpsimd)[j].dma_start(
                    out=planes[j][32 * q : 32 * q + 16, :].bitcast(F32),
                    in_=W_map_scales[4 * j : 4 * j + 4, 4 * q : 4 * q + 4, :].bitcast(F32),
                )

        pieces = {}

        def load(g0, n, b0, b1):
            wt = wpool.tile(
                [P, n, NB * (b1 - b0)], U32, name="w%d_%d" % (g0, b0), tag="w", align_bytes=64
            )
            nc.sync.dma_start(
                out=wt[:].bitcast(I32),
                in_=W_map_words[g0 : g0 + n]
                .rearrange("g p n t -> p g (n t)")[:, :, 4 * NB * b0 : 4 * NB * b1]
                .bitcast(I32),
            )
            for b in range(b0, b1):
                for gg in range(n):
                    pieces[(g0 + gg, b)] = wt[:, gg, NB * (b - b0) : NB * (b - b0 + 1)]

        for g in range(G):
            load(g, 1, 0, AB)
            if g == 0:
                nc.sync.dma_start(out=bstage[0:4, :], in_=b_map.rearrange("(j n) -> j n", j=4))

        def sorted_view(ap, g):
            return ap.rearrange("n (g p t) -> n g t p", g=g, p=P, t=4)

        def transposes(g0):
            tp = auxp.tile([P, 2, 4, P], BF16, name="tp%d" % g0, tag="aux")
            for gg in range(2):
                for t in range(4):
                    nc.tensor.transpose(tp[:, gg, t, :], hs[:, g0 + gg, t, :], ident[:])
            return tp

        def copy_out(tp, g0, engine):
            dst = grouped[:, g0 : g0 + 2]
            srcv = tp[:].rearrange("p g t n -> p g n t")
            if engine == "v":
                nc.vector.tensor_copy(out=dst, in_=srcv)
            else:
                nc.scalar.copy(out=dst, in_=srcv)

        def quantise(h):
            nc.vector.quantize_mx(
                out=hcodes[:, 4 * P * h : 4 * P * (h + 1)].bitcast(FP8X4),
                scales=hplanes[:, 4 * P * h : 4 * P * (h + 1)],
                in_=grouped[:, 4 * h : 4 * h + 4].rearrange("p g n t -> p (g n t)"),
            )

        tps = []
        for k in range(2):
            cols = slice(1024 * k, 1024 * (k + 1))
            nc.vector.tensor_tensor(
                out=hs[:, 2 * k : 2 * k + 2],
                in0=sorted_view(src_sb[:, 0, cols], 2),
                in1=sorted_view(src_sb[:, 1, cols], 2),
                op=ALU.add,
            )
            tps.append(transposes(2 * k))
        copy_out(tps[0], 0, "v")
        copy_out(tps[1], 2, "v")
        quantise(0)

        nc.vector.tensor_single_scalar(
            out=magbits[:], in_=neigh_sb[:].bitcast(I32), scalar=0x7FFF7FFF, op=ALU.bitwise_and
        )
        nc.vector.tensor_reduce(out=maxbits[:], in_=magbits[:], axis=mybir.AxisListType.X, op=ALU.max)
        nc.vector.tensor_tensor(out=nsum[:], in0=neigh_sb[:, 0, :], in1=neigh_sb[:, 1, :], op=ALU.add)
        nc.vector.tensor_single_scalar(out=valid[:], in_=maxbits[:], scalar=0.0, op=ALU.is_gt)
        nc.vector.tensor_scalar(
            out=num[:],
            in0=valid[:, 0:1],
            scalar1=valid[:, 1:2],
            scalar2=1.0,
            op0=ALU.add,
            op1=ALU.max,
        )
        nc.vector.reciprocal(out=rnum[:], in_=num[:])
        nc.vector.tensor_scalar(
            out=hs[:, 4:8], in0=sorted_view(nsum[:], 4), scalar1=rnum[:, 0:1], scalar2=None, op0=ALU.mult
        )

        def second_half():
            t4 = transposes(4)
            t6 = transposes(6)
            copy_out(t4, 4, "v")
            copy_out(t6, 6, "s")
            quantise(1)

        def bias_bank(i):
            bp = auxp.tile([P, NB], F32, name="bp%d" % i, tag="aux")
            j, c = i // 3, i % 3
            nc.tensor.matmul(
                out=bp[:],
                lhsT=ident[:, j : j + 1].to_broadcast([P, P]),
                rhs=bstage[:, NB * c : NB * (c + 1)],
                start=True,
                stop=True,
            )
            nc.scalar.copy(out=bias_sb[:, NB * i : NB * (i + 1)], in_=bp[:])

        def mx(acc, g, bank):
            k = 4 * (g % 4)
            nc.tensor.matmul_mx(
                out=acc[:],
                lhsT=hcodes[:, P * g : P * (g + 1)].bitcast(FP8X4),
                lhsT_scale=hplanes[:, P * g : P * (g + 1)],
                rhs=pieces[(g, bank)].bitcast(FP8X4),
                rhs_scale=planes[g // 4][k:P, NB * bank : NB * (bank + 1)],
                start=(g == 0),
                stop=(g == G - 1),
            )

        def add_bias(acc, bank):
            cols = slice(NB * bank, NB * (bank + 1))
            nc.vector.tensor_tensor(out=out_sb[:, cols], in0=acc[:], in1=bias_sb[:, cols], op=ALU.add)

        def leaky(c0, c1):
            nc.vector.scalar_tensor_tensor(
                out=out_sb[:, c0:c1],
                in0=out_sb[:, c0:c1],
                scalar=0.01,
                in1=out_sb[:, c0:c1],
                op0=ALU.mult,
                op1=ALU.max,
            )

        def store(c0, c1):
            nc.sync.dma_start(out=out[:, c0:c1], in_=out_sb[:, c0:c1])

        def finish(accs, bank):
            n = len(accs)
            for b in range(n + 1):
                if b < n:
                    add_bias(accs[b], bank + b)
                if b > 0:
                    leaky(NB * (bank + b - 1), NB * (bank + b))

        accs = [accp.tile([P, NB], F32, name="acc%d" % b, tag="acc") for b in range(PLAIN)]
        for g in range(G):
            if g == 4:
                second_half()
                accs += [auxp.tile([P, NB], F32, name="acc%d" % b, tag="aux") for b in range(PLAIN, AB)]
                for b in range(PLAIN, AB):
                    for gg in range(g):
                        mx(accs[b], gg, b)
            for b in range(len(accs)):
                mx(accs[b], g, b)
            if g < 4:
                for i in range(3):
                    bias_bank(3 * g + i)
            if g == 4:
                load(0, 2, AB, AB + BB)
                load(2, 2, AB, AB + BB)
                load(4, 2, AB, AB + BB)
                for b in range(AB, AB + BB, STAIR):
                    load(6, 2, b, b + STAIR)
        finish(accs, 0)
        store(0, AC)

        accs = [accp.tile([P, NB], F32, name="acc%d" % (AB + b), tag="acc") for b in range(BB)]
        for g0 in range(0, 6, 2):
            for b in range(BB):
                for g in range(g0, g0 + 2):
                    mx(accs[b], g, AB + b)
        for b0 in range(0, BB, STAIR):
            for b in range(b0, b0 + STAIR):
                for g in range(6, G):
                    mx(accs[b], g, AB + b)
            finish(accs[b0 : b0 + STAIR], AB + b0)
            if b0 + STAIR < BB:
                store(NB * (AB + b0), NB * (AB + b0 + STAIR))
            else:
                for b in range(AB + b0, AB + b0 + STAIR):
                    store(NB * b, NB * (b + 1))
